import numpy as np
import ml_dtypes


def mxq(x, axis, fmt="e4m3"):
    dtype, down = {"e4m3": (ml_dtypes.float8_e4m3fn, 7), "e5m2": (ml_dtypes.float8_e5m2, 14)}[fmt]
    v = np.moveaxis(np.asarray(x, np.float32).astype(ml_dtypes.bfloat16).astype(np.float64), axis, -1)
    blocks = v.reshape(v.shape[:-1] + (-1, 32))
    amax = np.abs(blocks).max(-1, keepdims=True)
    byte = np.maximum(np.where(amax > 0, np.frexp(amax)[1] - 1 + 127, 0) - down, 1)
    scale = np.exp2(byte - 127.0)
    codes = (blocks / scale).astype(np.float32).astype(dtype).astype(np.float64)
    return np.moveaxis((codes * scale).reshape(v.shape), -1, axis)


WIDE = False


def mx_kscale(k):
    if not WIDE:
        return np.ones(k)
    levels = np.array([10, -10, 5, -5, 0])
    a = np.random.permutation(np.resize(levels, k // 512 * 4)).reshape(k // 512, 4)
    idx = np.arange(k)
    return np.exp2(a[idx // 512, idx % 128 // 32])


BF16 = ml_dtypes.bfloat16


def bf(x):
    return np.asarray(x, np.float32).astype(BF16)


def f64(x):
    return np.asarray(x).astype(np.float64)


E2M1 = np.array([0.0, 0.5, 1.0, 1.5, 2.0, 3.0, 4.0, 6.0, -0.0, -0.5, -1.0, -1.5, -2.0, -3.0, -4.0, -6.0])


def pack_weight(w, fmt):
    k, n = w.shape
    w = f64(bf(w)).reshape(k // 32, 32, n)
    amax = np.abs(w).max(1)
    if fmt == "e4m3":
        byte = np.frexp(amax)[1] - 1 + 127 - 7
    else:
        mant, ex = np.frexp(amax / 6.0)
        byte = np.where(mant > 0.5, ex, ex - 1) + 127
    byte = np.clip(np.where(amax > 0, byte, 1), 1, 254)
    scaled = (w * np.exp2(127.0 - byte)[:, None, :]).reshape(k, n).astype(np.float32)
    by_word = np.ascontiguousarray(scaled.reshape(k // 512, 128, 4, n).transpose(0, 1, 3, 2))
    if fmt == "e4m3":
        words = by_word.astype(ml_dtypes.float8_e4m3fn).view(np.uint8)
    else:
        c = by_word.astype(ml_dtypes.float4_e2m1fn).view(np.uint8) & 0xF
        words = c[..., 0::2] | (c[..., 1::2] << 4)
    return np.ascontiguousarray(words), np.ascontiguousarray(byte.astype(np.uint8).reshape(k // 512, 16, n))


def unpack_weight(words, scales, fmt):
    g, p, n, _ = words.shape
    if fmt == "e4m3":
        vals = np.ascontiguousarray(words).view(ml_dtypes.float8_e4m3fn).astype(np.float64)
    else:
        nib = np.empty((g, p, n, 4), np.uint8)
        nib[..., 0::2] = words & 0xF
        nib[..., 1::2] = words >> 4
        vals = E2M1[nib]
    vals = vals * np.repeat(np.exp2(scales.astype(np.float64) - 127.0), 8, axis=1)[..., None]
    return vals.transpose(0, 1, 3, 2).reshape(g * 512, n)

def pack4(w):
    words, scales = pack_weight(w, "e2m1")
    return words.reshape(words.shape[0], 128, -1), scales


def unpack4(words, scales):
    return unpack_weight(words.reshape(words.shape[0], 128, -1, 2), scales, "e2m1")


B, D, H, F, K = 8192, 1024, 256, 1024, 128
EPS_LN = 1e-5


def silu(v):
    return v / (1.0 + np.exp(-v))


def setup_inputs():
    s = mx_kscale(D)
    x = bf(np.random.standard_normal((B, D)) * s)
    W1_words, W1_scales = pack4(np.random.standard_normal((D, H)) / np.sqrt(D) / s[:, None])
    return {"x": x,
            "W1_words": W1_words,
            "W1_scales": W1_scales,
            "b1": bf(0.2 * np.random.standard_normal(H)),
            "g": bf(1.0 + 0.1 * np.random.standard_normal(H)),
            "beta": bf(0.1 * np.random.standard_normal(H))}


def reference(x, W1_words, W1_scales, b1, g, beta):
    h = silu((mxq(f64(x), 1, "e4m3") @ unpack4(W1_words, W1_scales)) + f64(b1))
    mu = h.mean(-1, keepdims=True)
    var = ((h - mu) ** 2).mean(-1, keepdims=True)
    return (h - mu) / np.sqrt(var + EPS_LN) * f64(g) + f64(beta)

@@ -1,0 +1,217 @@
+from contextlib import ExitStack
+
+import concourse.masks as masks
+import concourse.mybir as mybir
+
+BF16 = mybir.dt.bfloat16
+F32 = mybir.dt.float32
+I32 = mybir.dt.int32
+U32 = mybir.dt.uint32
+U8 = mybir.dt.uint8
+FP8X4 = mybir.dt.float8_e4m3fn_x4
+FP4X4 = mybir.dt.float4_e2m1fn_x4
+ACT = mybir.ActivationFunctionType
+ALU = mybir.AluOpType
+
+P = 128
+B = 8192
+K = 1024
+H = 256
+EPS_LN = 1e-5
+
+GROUPS = K // (4 * P)
+WORDS = 2 * P
+N_PASS = 128
+HALVES = H // N_PASS
+TILES = 2
+ROUNDS = B // (TILES * P)
+LOADS_AHEAD = 4
+LAST_LAG = 4
+
+FLOPS = 2 * B * K * H
+
+
+def tile_evidentialhead_pa_t_kernel(tc, x, w_words_in, w_scales_in, b1, gain, shift, out):
+    nc = tc.nc
+    x_rounds = x.rearrange("(j p i) k -> j p i k", p=P, i=TILES)
+    out_rounds = out.rearrange("(j p i) n -> j p i n", p=P, i=TILES)
+
+    with ExitStack() as ctx:
+        const = ctx.enter_context(tc.tile_pool(name="const", bufs=1))
+        x_pool = ctx.enter_context(tc.tile_pool(name="x", bufs=LOADS_AHEAD + 2))
+        work = ctx.enter_context(tc.tile_pool(name="work", bufs=3))
+        stats = ctx.enter_context(tc.tile_pool(name="stats", bufs=6))
+        xt_pool = ctx.enter_context(tc.psum_pool(name="xt", bufs=2 * TILES))
+        acc_pool = ctx.enter_context(tc.psum_pool(name="acc", bufs=2))
+        ctx.enter_context(tc.manual_schedule())
+
+        x_of = [None] * ROUNDS
+        xt_of = [None] * ROUNDS
+        grouped_of = [None] * ROUNDS
+        codes_of = [None] * ROUNDS
+        acc_of = [None] * ROUNDS
+        z_of = [None] * ROUNDS
+        h_of = [None] * ROUNDS
+        moments_of = [None] * ROUNDS
+        centred_of = [None] * ROUNDS
+
+        def load(j):
+            x_sb = x_pool.tile([P, TILES, K], BF16)
+            nc.sync.dma_start(out=x_sb[:], in_=x_rounds[j])
+            x_of[j] = x_sb
+
+        def transpose(j):
+            banks = []
+            for i in range(TILES):
+                x_words = x_of[j][:, i, :].bitcast(F32)
+                xt = xt_pool.tile([P, GROUPS, 2, P], F32)
+                for g in range(GROUPS):
+                    for u in range(2):
+                        nc.tensor.transpose(
+                            xt[:, g, u, :], x_words[:, g * WORDS + u : (g + 1) * WORDS : 2], ident[:]
+                        )
+                banks.append(xt)
+            xt_of[j] = banks
+
+        def copy_out(j):
+            grouped = work.tile([P, TILES, K], BF16, align_bytes=64)
+            for i in range(TILES):
+                nc.scalar.copy(
+                    out=grouped[:, i, :].bitcast(F32).rearrange("p (g r u) -> p g r u", g=GROUPS, u=2),
+                    in_=xt_of[j][i][:].rearrange("p g u r -> p g r u"),
+                )
+            grouped_of[j] = grouped
+
+        def quantise(j):
+            codes = work.tile([P, TILES, GROUPS, P], U32, align_bytes=64)
+            scales = work.tile([P, TILES, GROUPS, P], U8, align_bytes=64)
+            nc.vector.quantize_mx(
+                out=codes[:].rearrange("p i g r -> p (i g r)").bitcast(FP8X4),
+                scales=scales[:].rearrange("p i g r -> p (i g r)"),
+                in_=grouped_of[j][:].rearrange("p i k -> p (i k)"),
+            )
+            codes_of[j] = (codes, scales)
+
+        def multiply(j):
+            codes, scales = codes_of[j]
+            acc = acc_pool.tile([P, TILES, H], F32)
+            for i in range(TILES):
+                for half in range(HALVES):
+                    cols = slice(half * N_PASS, (half + 1) * N_PASS)
+                    word_bytes = slice(half * 2 * N_PASS, (half + 1) * 2 * N_PASS)
+                    for g in range(GROUPS):
+                        nc.tensor.matmul_mx(
+                            out=acc[:, i, cols],
+                            lhsT=codes[:, i, g, :].bitcast(FP8X4),
+                            lhsT_scale=scales[:, i, g, :],
+                            rhs=w_words[:, g, word_bytes].bitcast(FP4X4),
+                            rhs_scale=w_scales[:, g, cols],
+                            start=(g == 0),
+                            stop=(g == GROUPS - 1),
+                        )
+            acc_of[j] = acc
+
+        def add_bias(j):
+            z = work.tile([P, TILES, H], F32)
+            nc.vector.tensor_tensor(
+                out=z[:], in0=acc_of[j][:], in1=b1_all[:].unsqueeze(1).to_broadcast([P, TILES, H]), op=ALU.add
+            )
+            z_of[j] = z
+
+        def silu_and_moments(j):
+            h = work.tile([P, TILES, H], F32)
+            h_sum = stats.tile([P, TILES], F32)
+            dev_sq = stats.tile([P, TILES], F32)
+            for i in range(TILES):
+                nc.scalar.activation(out=h[:, i, :], in_=z_of[j][:, i, :], func=ACT.Silu, accum_out=h_sum[:, i : i + 1])
+            for i in range(TILES):
+                squares = work.tile([P, H], BF16, bufs=4)
+                nc.scalar.activation(
+                    out=squares[:],
+                    in_=h[:, i, :],
+                    func=ACT.Square,
+                    scale=-float(H),
+                    bias=h_sum[:, i : i + 1],
+                    accum_out=dev_sq[:, i : i + 1],
+                )
+            mean = stats.tile([P, TILES], F32)
+            var_eps = stats.tile([P, TILES], F32)
+            rstd = stats.tile([P, TILES], F32)
+            nc.gpsimd.tensor_scalar(out=mean[:], in0=h_sum[:], scalar1=1.0 / H, scalar2=0.0, op0=ALU.mult, op1=ALU.add)
+            nc.gpsimd.tensor_scalar(
+                out=var_eps[:], in0=dev_sq[:], scalar1=1.0 / H**3, scalar2=EPS_LN, op0=ALU.mult, op1=ALU.add
+            )
+            nc.gpsimd.tensor_tensor(out=rstd[:], in0=var_eps[:], in1=minus_half[:], op=ALU.pow)
+            h_of[j] = h
+            moments_of[j] = (mean, rstd)
+
+        def centre_times_gain(j):
+            mean, rstd = moments_of[j]
+            centred = work.tile([P, TILES, H], F32)
+            for i in range(TILES):
+                nc.vector.scalar_tensor_tensor(
+                    out=centred[:, i, :],
+                    in0=h_of[j][:, i, :],
+                    scalar=mean[:, i : i + 1],
+                    in1=gain_all[:],
+                    op0=ALU.subtract,
+                    op1=ALU.mult,
+                )
+            centred_of[j] = centred
+
+        def scale_shift_store(j):
+            mean, rstd = moments_of[j]
+            result = work.tile([P, TILES, H], F32)
+            for i in range(TILES):
+                nc.vector.scalar_tensor_tensor(
+                    out=result[:, i, :],
+                    in0=centred_of[j][:, i, :],
+                    scalar=rstd[:, i : i + 1],
+                    in1=shift_all[:],
+                    op0=ALU.mult,
+                    op1=ALU.add,
+                )
+            nc.sync.dma_start(out=out_rounds[j], in_=result[:])
+
+        load(0)
+
+        w_words = const.tile([P, GROUPS, 2 * H], U8, align_bytes=64)
+        nc.sync.dma_start(out=w_words[:].bitcast(I32), in_=w_words_in.rearrange("g p b -> p g b").bitcast(I32))
+
+        w_scales = const.tile([P, GROUPS, H], U8, align_bytes=64)
+        nc.vector.memset(w_scales[:].rearrange("p g n -> p (g n)").bitcast(I32), 0)
+        for quad in range(4):
+            nc.sync.dma_start(
+                out=w_scales[32 * quad : 32 * quad + 4, :, :].bitcast(I32),
+                in_=w_scales_in[:, 4 * quad : 4 * quad + 4, :].rearrange("g r n -> r g n").bitcast(I32),
+            )
+
+        for j in range(1, LOADS_AHEAD):
+            load(j)
+
+        ident = const.tile([P, P], F32)
+        masks.make_identity(nc, ident[:])
+        minus_half = const.tile([P, TILES], F32)
+        nc.gpsimd.memset(minus_half[:], -0.5)
+
+        b1_all = const.tile([P, H], BF16)
+        gain_all = const.tile([P, H], BF16)
+        shift_all = const.tile([P, H], BF16)
+        nc.scalar.dma_start(out=b1_all[:], in_=b1.partition_broadcast(P))
+        nc.scalar.dma_start(out=gain_all[:], in_=gain.partition_broadcast(P))
+        nc.scalar.dma_start(out=shift_all[:], in_=shift.partition_broadcast(P))
+
+        def stage(work_on, j):
+            if 0 <= j < ROUNDS:
+                work_on(j)
+
+        for t in range(ROUNDS + LAST_LAG):
+            stage(load, t + LOADS_AHEAD)
+            stage(transpose, t)
+            stage(copy_out, t)
+            stage(multiply, t - 1)
+            stage(silu_and_moments, t - 2)
+            stage(centre_times_gain, t - 3)
+            stage(scale_shift_store, t - LAST_LAG)
+            stage(quantise, t)
+            stage(add_bias, t - 1)

@@ -43,6 +43,7 @@ def tile_evidentialhead_pa_t_kernel(tc, x, w_words_in, w_scales_in, b1, gain, sh
         stats = ctx.enter_context(tc.tile_pool(name="stats", bufs=6))
         xt_pool = ctx.enter_context(tc.psum_pool(name="xt", bufs=2 * TILES))
         acc_pool = ctx.enter_context(tc.psum_pool(name="acc", bufs=2))
+        spread_pool = ctx.enter_context(tc.psum_pool(name="spread", bufs=1))
         ctx.enter_context(tc.manual_schedule())
 
         x_of = [None] * ROUNDS
@@ -94,7 +95,7 @@ def tile_evidentialhead_pa_t_kernel(tc, x, w_words_in, w_scales_in, b1, gain, sh
 
         def multiply(j):
             codes, scales = codes_of[j]
-            acc = acc_pool.tile([P, TILES, H], F32)
+            acc = acc_pool.tile([P, TILES, H], F32, tag="acc")
             for i in range(TILES):
                 for half in range(HALVES):
                     cols = slice(half * N_PASS, (half + 1) * N_PASS)
@@ -153,7 +154,7 @@ def tile_evidentialhead_pa_t_kernel(tc, x, w_words_in, w_scales_in, b1, gain, sh
                     out=centred[:, i, :],
                     in0=h_of[j][:, i, :],
                     scalar=mean[:, i : i + 1],
-                    in1=gain_all[:],
+                    in1=gain_shift[:, 0, :],
                     op0=ALU.subtract,
                     op1=ALU.mult,
                 )
@@ -167,7 +168,7 @@ def tile_evidentialhead_pa_t_kernel(tc, x, w_words_in, w_scales_in, b1, gain, sh
                     out=result[:, i, :],
                     in0=centred_of[j][:, i, :],
                     scalar=rstd[:, i : i + 1],
-                    in1=shift_all[:],
+                    in1=gain_shift[:, 1, :],
                     op0=ALU.mult,
                     op1=ALU.add,
                 )
@@ -194,12 +195,18 @@ def tile_evidentialhead_pa_t_kernel(tc, x, w_words_in, w_scales_in, b1, gain, sh
         minus_half = const.tile([P, TILES], F32)
         nc.gpsimd.memset(minus_half[:], -0.5)
 
-        b1_all = const.tile([P, H], BF16)
-        gain_all = const.tile([P, H], BF16)
-        shift_all = const.tile([P, H], BF16)
-        nc.scalar.dma_start(out=b1_all[:], in_=b1.partition_broadcast(P))
-        nc.scalar.dma_start(out=gain_all[:], in_=gain.partition_broadcast(P))
-        nc.scalar.dma_start(out=shift_all[:], in_=shift.partition_broadcast(P))
+        rows = const.tile([P, 3, H], BF16)
+        nc.vector.memset(rows[:].rearrange("p v n -> p (v n)").bitcast(I32), 0)
+        for v, vector in enumerate((b1, gain, shift)):
+            nc.scalar.dma_start(out=rows[0:1, v, :], in_=vector.rearrange("(o n) -> o n", o=1))
+        ones = const.tile([P, P], BF16)
+        nc.vector.memset(ones[:], 1.0)
+        gain_shift = spread_pool.tile([P, 2, H], F32)
+        nc.tensor.matmul(out=gain_shift[:], lhsT=ones[:], rhs=rows[:, 1:3, :], start=True, stop=True)
+        b1_bank = acc_pool.tile([P, TILES, H], F32, tag="acc")
+        nc.tensor.matmul(out=b1_bank[:, 0, :], lhsT=ones[:], rhs=rows[:, 0, :], start=True, stop=True)
+        b1_all = const.tile([P, H], F32)
+        nc.vector.tensor_copy(out=b1_all[:], in_=b1_bank[:, 0, :])
 
         def stage(work_on, j):
             if 0 <= j < ROUNDS:

@@ -27,6 +27,7 @@ TILES = 2
 ROUNDS = B // (TILES * P)
 LOADS_AHEAD = 4
 LAST_LAG = 4
+VECTOR_COPY_ROUNDS = (0, 2, 3)
 
 FLOPS = 2 * B * K * H
 
@@ -77,7 +78,9 @@ def tile_evidentialhead_pa_t_kernel(tc, x, w_words_in, w_scales_in, b1, gain, sh
         def copy_out(j):
             grouped = work.tile([P, TILES, K], BF16, align_bytes=64)
             for i in range(TILES):
-                nc.scalar.copy(
+                by_vector = i == TILES - 1 and j in VECTOR_COPY_ROUNDS
+                copy = nc.vector.tensor_copy if by_vector else nc.scalar.copy
+                copy(
                     out=grouped[:, i, :].bitcast(F32).rearrange("p (g r u) -> p g r u", g=GROUPS, u=2),
                     in_=xt_of[j][i][:].rearrange("p g u r -> p g r u"),
                 )

@@ -178,6 +178,7 @@ def tile_evidentialhead_pa_t_kernel(tc, x, w_words_in, w_scales_in, b1, gain, sh
             nc.sync.dma_start(out=out_rounds[j], in_=result[:])
 
         load(0)
+        load(1)
 
         w_words = const.tile([P, GROUPS, 2 * H], U8, align_bytes=64)
         nc.sync.dma_start(out=w_words[:].bitcast(I32), in_=w_words_in.rearrange("g p b -> p g b").bitcast(I32))
@@ -190,7 +191,7 @@ def tile_evidentialhead_pa_t_kernel(tc, x, w_words_in, w_scales_in, b1, gain, sh
                 in_=w_scales_in[:, 4 * quad : 4 * quad + 4, :].rearrange("g r n -> r g n").bitcast(I32),
             )
 
-        for j in range(1, LOADS_AHEAD):
+        for j in range(2, LOADS_AHEAD):
             load(j)
 
         ident = const.tile([P, P], F32)
@@ -204,12 +205,6 @@ def tile_evidentialhead_pa_t_kernel(tc, x, w_words_in, w_scales_in, b1, gain, sh
             nc.scalar.dma_start(out=rows[0:1, v, :], in_=vector.rearrange("(o n) -> o n", o=1))
         ones = const.tile([P, P], BF16)
         nc.vector.memset(ones[:], 1.0)
-        gain_shift = spread_pool.tile([P, 2, H], F32)
-        nc.tensor.matmul(out=gain_shift[:], lhsT=ones[:], rhs=rows[:, 1:3, :], start=True, stop=True)
-        b1_bank = acc_pool.tile([P, TILES, H], F32, tag="acc")
-        nc.tensor.matmul(out=b1_bank[:, 0, :], lhsT=ones[:], rhs=rows[:, 0, :], start=True, stop=True)
-        b1_all = const.tile([P, H], F32)
-        nc.vector.tensor_copy(out=b1_all[:], in_=b1_bank[:, 0, :])
 
         def stage(work_on, j):
             if 0 <= j < ROUNDS:
@@ -224,4 +219,11 @@ def tile_evidentialhead_pa_t_kernel(tc, x, w_words_in, w_scales_in, b1, gain, sh
             stage(centre_times_gain, t - 3)
             stage(scale_shift_store, t - LAST_LAG)
             stage(quantise, t)
+            if t == 0:
+                gain_shift = spread_pool.tile([P, 2, H], F32)
+                nc.tensor.matmul(out=gain_shift[:], lhsT=ones[:], rhs=rows[:, 1:3, :], start=True, stop=True)
+                b1_bank = acc_pool.tile([P, TILES, H], F32, tag="acc")
+                nc.tensor.matmul(out=b1_bank[:, 0, :], lhsT=ones[:], rhs=rows[:, 0, :], start=True, stop=True)
+                b1_all = const.tile([P, H], F32)
+                nc.vector.tensor_copy(out=b1_all[:], in_=b1_bank[:, 0, :])
             stage(add_bias, t - 1)

from contextlib import ExitStack

import concourse.masks as masks
import concourse.mybir as mybir

BF16 = mybir.dt.bfloat16
F32 = mybir.dt.float32
I32 = mybir.dt.int32
U32 = mybir.dt.uint32
U8 = mybir.dt.uint8
FP8X4 = mybir.dt.float8_e4m3fn_x4
FP4X4 = mybir.dt.float4_e2m1fn_x4
ACT = mybir.ActivationFunctionType
ALU = mybir.AluOpType

P = 128
B = 8192
K = 1024
H = 256
EPS_LN = 1e-5

GROUPS = K // (4 * P)
WORDS = 2 * P
N_PASS = 128
HALVES = H // N_PASS
TILES = 2
ROUNDS = B // (TILES * P)
LOADS_AHEAD = 4
LAST_LAG = 4
VECTOR_COPY_ROUNDS = (0, 2, 3)

FLOPS = 2 * B * K * H


def tile_evidentialhead_pa_t_kernel(tc, x, w_words_in, w_scales_in, b1, gain, shift, out):
    nc = tc.nc
    x_rounds = x.rearrange("(j p i) k -> j p i k", p=P, i=TILES)
    out_rounds = out.rearrange("(j p i) n -> j p i n", p=P, i=TILES)

    with ExitStack() as ctx:
        const = ctx.enter_context(tc.tile_pool(name="const", bufs=1))
        x_pool = ctx.enter_context(tc.tile_pool(name="x", bufs=LOADS_AHEAD + 2))
        work = ctx.enter_context(tc.tile_pool(name="work", bufs=3))
        stats = ctx.enter_context(tc.tile_pool(name="stats", bufs=6))
        xt_pool = ctx.enter_context(tc.psum_pool(name="xt", bufs=2 * TILES))
        acc_pool = ctx.enter_context(tc.psum_pool(name="acc", bufs=2))
        spread_pool = ctx.enter_context(tc.psum_pool(name="spread", bufs=1))
        ctx.enter_context(tc.manual_schedule())

        x_of = [None] * ROUNDS
        xt_of = [None] * ROUNDS
        grouped_of = [None] * ROUNDS
        codes_of = [None] * ROUNDS
        acc_of = [None] * ROUNDS
        z_of = [None] * ROUNDS
        h_of = [None] * ROUNDS
        moments_of = [None] * ROUNDS
        centred_of = [None] * ROUNDS

        def load(j):
            x_sb = x_pool.tile([P, TILES, K], BF16)
            nc.sync.dma_start(out=x_sb[:], in_=x_rounds[j])
            x_of[j] = x_sb

        def transpose(j):
            banks = []
            for i in range(TILES):
                x_words = x_of[j][:, i, :].bitcast(F32)
                xt = xt_pool.tile([P, GROUPS, 2, P], F32)
                for g in range(GROUPS):
                    for u in range(2):
                        nc.tensor.transpose(
                            xt[:, g, u, :], x_words[:, g * WORDS + u : (g + 1) * WORDS : 2], ident[:]
                        )
                banks.append(xt)
            xt_of[j] = banks

        def copy_out(j):
            grouped = work.tile([P, TILES, K], BF16, align_bytes=64)
            for i in range(TILES):
                by_vector = i == TILES - 1 and j in VECTOR_COPY_ROUNDS
                copy = nc.vector.tensor_copy if by_vector else nc.scalar.copy
                copy(
                    out=grouped[:, i, :].bitcast(F32).rearrange("p (g r u) -> p g r u", g=GROUPS, u=2),
                    in_=xt_of[j][i][:].rearrange("p g u r -> p g r u"),
                )
            grouped_of[j] = grouped

        def quantise(j):
            codes = work.tile([P, TILES, GROUPS, P], U32, align_bytes=64)
            scales = work.tile([P, TILES, GROUPS, P], U8, align_bytes=64)
            nc.vector.quantize_mx(
                out=codes[:].rearrange("p i g r -> p (i g r)").bitcast(FP8X4),
                scales=scales[:].rearrange("p i g r -> p (i g r)"),
                in_=grouped_of[j][:].rearrange("p i k -> p (i k)"),
            )
            codes_of[j] = (codes, scales)

        def multiply(j):
            codes, scales = codes_of[j]
            acc = acc_pool.tile([P, TILES, H], F32, tag="acc")
            for i in range(TILES):
                for half in range(HALVES):
                    cols = slice(half * N_PASS, (half + 1) * N_PASS)
                    word_bytes = slice(half * 2 * N_PASS, (half + 1) * 2 * N_PASS)
                    for g in range(GROUPS):
                        nc.tensor.matmul_mx(
                            out=acc[:, i, cols],
                            lhsT=codes[:, i, g, :].bitcast(FP8X4),
                            lhsT_scale=scales[:, i, g, :],
                            rhs=w_words[:, g, word_bytes].bitcast(FP4X4),
                            rhs_scale=w_scales[:, g, cols],
                            start=(g == 0),
                            stop=(g == GROUPS - 1),
                        )
            acc_of[j] = acc

        def add_bias(j):
            z = work.tile([P, TILES, H], F32)
            nc.vector.tensor_tensor(
                out=z[:], in0=acc_of[j][:], in1=b1_all[:].unsqueeze(1).to_broadcast([P, TILES, H]), op=ALU.add
            )
            z_of[j] = z

        def silu_and_moments(j):
            h = work.tile([P, TILES, H], F32)
            h_sum = stats.tile([P, TILES], F32)
            dev_sq = stats.tile([P, TILES], F32)
            for i in range(TILES):
                nc.scalar.activation(out=h[:, i, :], in_=z_of[j][:, i, :], func=ACT.Silu, accum_out=h_sum[:, i : i + 1])
            for i in range(TILES):
                squares = work.tile([P, H], BF16, bufs=4)
                nc.scalar.activation(
                    out=squares[:],
                    in_=h[:, i, :],
                    func=ACT.Square,
                    scale=-float(H),
                    bias=h_sum[:, i : i + 1],
                    accum_out=dev_sq[:, i : i + 1],
                )
            mean = stats.tile([P, TILES], F32)
            var_eps = stats.tile([P, TILES], F32)
            rstd = stats.tile([P, TILES], F32)
            nc.gpsimd.tensor_scalar(out=mean[:], in0=h_sum[:], scalar1=1.0 / H, scalar2=0.0, op0=ALU.mult, op1=ALU.add)
            nc.gpsimd.tensor_scalar(
                out=var_eps[:], in0=dev_sq[:], scalar1=1.0 / H**3, scalar2=EPS_LN, op0=ALU.mult, op1=ALU.add
            )
            nc.gpsimd.tensor_tensor(out=rstd[:], in0=var_eps[:], in1=minus_half[:], op=ALU.pow)
            h_of[j] = h
            moments_of[j] = (mean, rstd)

        def centre_times_gain(j):
            mean, rstd = moments_of[j]
            centred = work.tile([P, TILES, H], F32)
            for i in range(TILES):
                nc.vector.scalar_tensor_tensor(
                    out=centred[:, i, :],
                    in0=h_of[j][:, i, :],
                    scalar=mean[:, i : i + 1],
                    in1=gain_shift[:, 0, :],
                    op0=ALU.subtract,
                    op1=ALU.mult,
                )
            centred_of[j] = centred

        def scale_shift_store(j):
            mean, rstd = moments_of[j]
            result = work.tile([P, TILES, H], F32)
            for i in range(TILES):
                nc.vector.scalar_tensor_tensor(
                    out=result[:, i, :],
                    in0=centred_of[j][:, i, :],
                    scalar=rstd[:, i : i + 1],
                    in1=gain_shift[:, 1, :],
                    op0=ALU.mult,
                    op1=ALU.add,
                )
            nc.sync.dma_start(out=out_rounds[j], in_=result[:])

        load(0)
        load(1)

        w_words = const.tile([P, GROUPS, 2 * H], U8, align_bytes=64)
        nc.sync.dma_start(out=w_words[:].bitcast(I32), in_=w_words_in.rearrange("g p b -> p g b").bitcast(I32))

        w_scales = const.tile([P, GROUPS, H], U8, align_bytes=64)
        nc.vector.memset(w_scales[:].rearrange("p g n -> p (g n)").bitcast(I32), 0)
        for quad in range(4):
            nc.sync.dma_start(
                out=w_scales[32 * quad : 32 * quad + 4, :, :].bitcast(I32),
                in_=w_scales_in[:, 4 * quad : 4 * quad + 4, :].rearrange("g r n -> r g n").bitcast(I32),
            )

        for j in range(2, LOADS_AHEAD):
            load(j)

        ident = const.tile([P, P], F32)
        masks.make_identity(nc, ident[:])
        minus_half = const.tile([P, TILES], F32)
        nc.gpsimd.memset(minus_half[:], -0.5)

        rows = const.tile([P, 3, H], BF16)
        nc.vector.memset(rows[:].rearrange("p v n -> p (v n)").bitcast(I32), 0)
        for v, vector in enumerate((b1, gain, shift)):
            nc.scalar.dma_start(out=rows[0:1, v, :], in_=vector.rearrange("(o n) -> o n", o=1))
        ones = const.tile([P, P], BF16)
        nc.vector.memset(ones[:], 1.0)

        def stage(work_on, j):
            if 0 <= j < ROUNDS:
                work_on(j)

        for t in range(ROUNDS + LAST_LAG):
            stage(load, t + LOADS_AHEAD)
            stage(transpose, t)
            stage(copy_out, t)
            stage(multiply, t - 1)
            stage(silu_and_moments, t - 2)
            stage(centre_times_gain, t - 3)
            stage(scale_shift_store, t - LAST_LAG)
            stage(quantise, t)
            if t == 0:
                gain_shift = spread_pool.tile([P, 2, H], F32)
                nc.tensor.matmul(out=gain_shift[:], lhsT=ones[:], rhs=rows[:, 1:3, :], start=True, stop=True)
                b1_bank = acc_pool.tile([P, TILES, H], F32, tag="acc")
                nc.tensor.matmul(out=b1_bank[:, 0, :], lhsT=ones[:], rhs=rows[:, 0, :], start=True, stop=True)
                b1_all = const.tile([P, H], F32)
                nc.vector.tensor_copy(out=b1_all[:], in_=b1_bank[:, 0, :])
            stage(add_bias, t - 1)
